import numpy as np
import ml_dtypes


def mxq(x, axis, fmt="e4m3"):
    dtype, down = {"e4m3": (ml_dtypes.float8_e4m3fn, 7), "e5m2": (ml_dtypes.float8_e5m2, 14)}[fmt]
    v = np.moveaxis(np.asarray(x, np.float32).astype(ml_dtypes.bfloat16).astype(np.float64), axis, -1)
    blocks = v.reshape(v.shape[:-1] + (-1, 32))
    amax = np.abs(blocks).max(-1, keepdims=True)
    byte = np.maximum(np.where(amax > 0, np.frexp(amax)[1] - 1 + 127, 0) - down, 1)
    scale = np.exp2(byte - 127.0)
    codes = (blocks / scale).astype(np.float32).astype(dtype).astype(np.float64)
    return np.moveaxis((codes * scale).reshape(v.shape), -1, axis)


WIDE = False


def mx_kscale(k):
    if not WIDE:
        return np.ones(k)
    levels = np.array([10, -10, 5, -5, 0])
    if k % 512:
        return np.exp2(np.random.permutation(np.resize(levels, k // 32))).repeat(32)
    a = np.empty((k // 512, 16))
    for p in range(k // 512):
        a[p, :8] = np.random.permutation(np.resize(levels, 8))
        for g in range(8):
            far = levels[np.abs(levels - a[p, g]) >= 10]
            a[p, g + 8] = far[np.random.randint(len(far))]
    return np.exp2(a.ravel()).repeat(32)


BF16 = ml_dtypes.bfloat16


def bf(x):
    return np.asarray(x, np.float32).astype(BF16)


def f64(x):
    return np.asarray(x).astype(np.float64)


E2M1 = np.array([0.0, 0.5, 1.0, 1.5, 2.0, 3.0, 4.0, 6.0, -0.0, -0.5, -1.0, -1.5, -2.0, -3.0, -4.0, -6.0])


def pack_weight(w, fmt):
    k, n = w.shape
    w = f64(bf(w)).reshape(k // 32, 32, n)
    amax = np.abs(w).max(1)
    if fmt == "e4m3":
        byte = np.frexp(amax)[1] - 1 + 127 - 7
    else:
        mant, ex = np.frexp(amax / 6.0)
        byte = np.where(mant > 0.5, ex, ex - 1) + 127
    byte = np.clip(np.where(amax > 0, byte, 1), 1, 254)
    scaled = (w * np.exp2(127.0 - byte)[:, None, :]).reshape(k, n).astype(np.float32)
    by_word = np.ascontiguousarray(scaled.reshape(k // 512, 128, 4, n).transpose(0, 1, 3, 2))
    if fmt == "e4m3":
        words = by_word.astype(ml_dtypes.float8_e4m3fn).view(np.uint8)
    else:
        c = by_word.astype(ml_dtypes.float4_e2m1fn).view(np.uint8) & 0xF
        words = c[..., 0::2] | (c[..., 1::2] << 4)
    return np.ascontiguousarray(words), np.ascontiguousarray(byte.astype(np.uint8).reshape(k // 512, 16, n))


def unpack_weight(words, scales, fmt):
    g, p, n, _ = words.shape
    if fmt == "e4m3":
        vals = np.ascontiguousarray(words).view(ml_dtypes.float8_e4m3fn).astype(np.float64)
    else:
        nib = np.empty((g, p, n, 4), np.uint8)
        nib[..., 0::2] = words & 0xF
        nib[..., 1::2] = words >> 4
        vals = E2M1[nib]
    vals = vals * np.repeat(np.exp2(scales.astype(np.float64) - 127.0), 8, axis=1)[..., None]
    return vals.transpose(0, 1, 3, 2).reshape(g * 512, n)


B, C, T, P, N, D = 8, 16, 2048, 128, 8, 512
L = T // P
G = L // N


def draw0():
    s = mx_kscale(D)
    u = mx_kscale(P * N)
    un = u.reshape(P, N).T
    ut = np.tile(u, G)
    h_enc = bf(np.random.standard_normal((N, B, C, G, D)) * 0.7 * s)
    dec_W = bf(np.random.standard_normal((N, D, P)) / np.sqrt(D) / s[None, :, None] * un[:, None, :])
    dec_b = bf(np.random.standard_normal((N, P)) * 0.2 * un)
    map_W_words, map_W_scales = pack_weight(np.random.standard_normal((T, T)) / np.sqrt(T) / ut[:, None], 'e4m3')
    map_b = bf(np.random.standard_normal(T) * 0.2)
    return {'h_enc': h_enc,
            'dec_W': dec_W,
            'dec_b': dec_b,
            'map_W_words': map_W_words,
            'map_W_scales': map_W_scales,
            'map_b': map_b}


def core(h_enc, dec_W, dec_b, map_W_words, map_W_scales, map_b):
    h = f64(h_enc).reshape(N, B * C * G, D)
    r = (mxq(h, 2, 'e4m3') @ mxq(f64(dec_W), 1, 'e4m3')) + f64(dec_b)[:, None, :]
    r = r.reshape(N, B, C, G * P)
    x_rec = np.moveaxis(r, 0, -1).reshape(B * C, T)
    y_hat = (mxq(x_rec, 1, 'e4m3') @ unpack_weight(map_W_words, map_W_scales, 'e4m3')) + f64(map_b)
    return y_hat.reshape(B, C, T)


def e4m3fn_bytes(y):
    return np.clip(np.asarray(y, np.float64), -448.0, 448.0).astype(np.float32).astype(ml_dtypes.float8_e4m3fn).view(np.uint8)


def e4m3fn_values(b):
    return np.asarray(b, np.uint8).view(ml_dtypes.float8_e4m3fn).astype(np.float64)


def setup_inputs():
    d = draw0()
    x0 = np.asarray(d['h_enc']).astype(np.float64)
    s = (np.max(np.abs(x0), axis=(0, 1, 2, 3), keepdims=True) / 448.0).astype(np.float32)
    out = {}
    for k, v in d.items():
        if k == 'h_enc':
            out['h_enc_bytes'] = e4m3fn_bytes(x0 / s.astype(np.float64))
            out['h_enc_scale'] = s
        else:
            out[k] = v
    return out


def reference(h_enc_bytes, h_enc_scale, dec_W, dec_b, map_W_words, map_W_scales, map_b):
    return core(e4m3fn_values(h_enc_bytes) * h_enc_scale.astype(np.float64), dec_W, dec_b, map_W_words, map_W_scales, map_b)

@@ -1,0 +1,244 @@
+from contextlib import ExitStack
+
+import concourse.mybir as mybir
+from concourse.masks import make_identity
+
+F32 = mybir.dt.float32
+BF16 = mybir.dt.bfloat16
+I32 = mybir.dt.int32
+U32 = mybir.dt.uint32
+U8 = mybir.dt.uint8
+FP8 = mybir.dt.float8_e4m3fn
+FP8X4 = mybir.dt.float8_e4m3fn_x4
+MULT = mybir.AluOpType.mult
+ADD = mybir.AluOpType.add
+
+P = 128
+MODELS = 8
+D = 512
+T = 2048
+BC = 128
+PATCHES = 2
+GROUPS = T // 512
+HALF = 64
+
+FLOPS = 2 * MODELS * BC * PATCHES * D * P + 2 * BC * T * T
+
+
+def tile_model_pb_w8_kernel(tc, h_bytes, h_scale, dec_W, dec_b, map_W_words, map_W_scales, map_b, out):
+    nc = tc.nc
+
+    with ExitStack() as ctx:
+        keep = ctx.enter_context(tc.tile_pool(name="keep", bufs=1))
+        psum = ctx.enter_context(tc.psum_pool(name="psum", bufs=1))
+        ctx.enter_context(tc.manual_schedule())
+
+        def sb(shape, dtype, name):
+            return keep.tile(shape, dtype, name=name, align_bytes=64)
+
+        def bank(i, shape, name):
+            return psum.tile(shape, F32, name=name, tag="bank%d" % i)
+
+        scale = sb([P, 2, D], F32, "scale")
+        nc.sync.dma_start(out=scale[:, 0], in_=h_scale.rearrange("a b c d k -> (a b c d k)").partition_broadcast(P))
+        nc.scalar.copy(out=scale[:, 1], in_=scale[:, 0])
+
+        h_view = h_bytes.rearrange("n b c l d -> (b c) l n d")
+        hb = {}
+        w_raw = {}
+
+        def load_h(u0, u1):
+            l, n0 = u0 // 4, 2 * (u0 % 4)
+            t = sb([P, 2 * (u1 - u0), D], U8, "hb%d" % u0)
+            nc.sync.dma_start(out=t[:], in_=h_view[:, l, n0 : n0 + 2 * (u1 - u0)])
+            for u in range(u0, u1):
+                hb[u] = t[:, 2 * (u - u0) : 2 * (u - u0) + 2]
+
+        def load_w(n0):
+            t = sb([P, 2, 4, P], BF16, "w_raw%d" % n0)
+            nc.sync.dma_start(out=t[:], in_=dec_W[n0 : n0 + 2].rearrange("n (p j) w -> p n j w", j=4))
+            w_raw[n0 // 2] = t
+
+        load_h(0, 1)
+        load_w(0)
+        load_h(1, 2)
+        load_w(2)
+        load_h(2, 4)
+        load_w(4)
+        load_w(6)
+        load_h(4, 8)
+
+        ident = sb([P, P], F32, "ident")
+        make_identity(nc, ident[:])
+        wsc = sb([P, T], U8, "wsc")
+        nc.gpsimd.memset(wsc[:].bitcast(I32), 0)
+        for q in range(4):
+            nc.sync.dma_start(
+                out=wsc[32 * q : 32 * q + 16, :].bitcast(I32),
+                in_=map_W_scales[:, 4 * q : 4 * q + 4, :].bitcast(I32),
+            )
+        dec_bias = sb([P, MODELS, P], BF16, "dec_bias")
+        nc.sync.dma_start(
+            out=dec_bias[:].rearrange("b n p -> b (n p)"),
+            in_=dec_b.rearrange("n p -> (n p)").partition_broadcast(P),
+        )
+        ww = []
+        for g in range(GROUPS):
+            t = sb([P, T], I32, "ww%d" % g)
+            nc.sync.dma_start(out=t[:], in_=map_W_words[g].rearrange("p n t -> p (n t)").bitcast(I32))
+            ww.append(t)
+        map_bias = sb([P, T], BF16, "map_bias")
+        nc.sync.dma_start(out=map_bias[:], in_=map_b.partition_broadcast(P))
+
+        hx, ht, hg, hc, hs = {}, {}, {}, {}, {}
+        wg, wc, ws = {}, {}, {}
+        x_ps, xb, xt, xg, xc, xs = {}, {}, {}, {}, {}, {}
+        acc = {}
+
+        def widen(u):
+            hx[u] = sb([P, 2, D], BF16, "hx%d" % u)
+            nc.vector.tensor_tensor(
+                out=hx[u][:].rearrange("b i d -> b (i d)"),
+                in0=hb[u].rearrange("b i d -> b (i d)").bitcast(FP8),
+                in1=scale[:].rearrange("b i d -> b (i d)"),
+                op=MULT,
+            )
+
+        def turn(u):
+            ht[u] = bank(u % 4, [P, 2, 2, P], "ht%d" % u)
+            for i in range(2):
+                words = hx[u][:, i].bitcast(F32)
+                for e in range(2):
+                    nc.tensor.transpose(ht[u][:, i, e], words[:, e::2], ident[:])
+
+        def h_out(u):
+            hg[u] = sb([P, 2, P, 4], BF16, "hg%d" % u)
+            nc.scalar.copy(
+                out=hg[u][:].rearrange("p i r k -> p (i r k)").bitcast(F32).rearrange("p (i r e) -> p i r e", i=2, e=2),
+                in_=ht[u][:].rearrange("p i e r -> p i r e"),
+            )
+
+        def h_quant(u):
+            hc[u] = sb([P, 2 * P], U32, "hc%d" % u)
+            hs[u] = sb([P, 2 * P], U8, "hs%d" % u)
+            nc.vector.quantize_mx(out=hc[u][:].bitcast(FP8X4), scales=hs[u][:], in_=hg[u][:].rearrange("p i r k -> p (i r k)"))
+
+        def w_group(j):
+            wg[j] = sb([P, 2, P, 4], BF16, "wg%d" % j)
+            nc.scalar.copy(out=wg[j][:], in_=w_raw[j][:].rearrange("p n j w -> p n w j"))
+
+        def w_quant(j):
+            wc[j] = sb([P, 2 * P], U32, "wc%d" % j)
+            ws[j] = sb([P, 2 * P], U8, "ws%d" % j)
+            nc.vector.quantize_mx(out=wc[j][:].bitcast(FP8X4), scales=ws[j][:], in_=wg[j][:].rearrange("p i r k -> p (i r k)"))
+
+        def decode(l, models):
+            for half in range(2):
+                g = 2 * l + half
+                if g not in x_ps:
+                    x_ps[g] = bank(4 + half, [P, MODELS, HALF], "x_ps%d" % g)
+                for n in models:
+                    u, i = 4 * l + n // 2, n % 2
+                    cols = slice(i * P + half * HALF, i * P + half * HALF + HALF)
+                    nc.tensor.matmul_mx(
+                        out=x_ps[g][:, n],
+                        lhsT=hc[u][:, i * P : (i + 1) * P].bitcast(FP8X4),
+                        lhsT_scale=hs[u][:, i * P : (i + 1) * P],
+                        rhs=wc[n // 2][:, cols].bitcast(FP8X4),
+                        rhs_scale=ws[n // 2][:, cols],
+                        start=True,
+                        stop=True,
+                    )
+
+        def x_bias(g):
+            half = g % 2
+            xb[g] = sb([P, HALF, MODELS], BF16, "xb%d" % g)
+            nc.vector.tensor_tensor(
+                out=xb[g][:],
+                in0=x_ps[g][:].rearrange("b n p -> b p n"),
+                in1=dec_bias[:, :, half * HALF : (half + 1) * HALF].rearrange("b n p -> b p n"),
+                op=ADD,
+            )
+
+        def x_turn(g):
+            xt[g] = bank(6 + g % 2, [P, 2, P], "xt%d" % g)
+            words = xb[g][:].rearrange("b p n -> b (p n)").bitcast(F32)
+            for e in range(2):
+                nc.tensor.transpose(xt[g][:, e], words[:, e::2], ident[:])
+
+        def x_out(g):
+            xg[g] = sb([P, P, 4], BF16, "xg%d" % g)
+            nc.scalar.copy(
+                out=xg[g][:].rearrange("p r k -> p (r k)").bitcast(F32).rearrange("p (r e) -> p r e", e=2),
+                in_=xt[g][:].rearrange("p e r -> p r e"),
+            )
+
+        def x_quant(g):
+            xc[g] = sb([P, P], U32, "xc%d" % g)
+            xs[g] = sb([P, P], U8, "xs%d" % g)
+            nc.vector.quantize_mx(out=xc[g][:].bitcast(FP8X4), scales=xs[g][:], in_=xg[g][:].rearrange("p r k -> p (r k)"))
+
+        def time_map(g):
+            for s in (3, 0, 1, 2):
+                if g == 0:
+                    acc[s] = bank(s, [P, 512], "acc%d" % s)
+                cols = slice(512 * s, 512 * (s + 1))
+                nc.tensor.matmul_mx(
+                    out=acc[s][:],
+                    lhsT=xc[g][:].bitcast(FP8X4),
+                    lhsT_scale=xs[g][:],
+                    rhs=ww[g][:, cols].bitcast(FP8X4),
+                    rhs_scale=wsc[4 * g : P, cols],
+                    start=(g == 0),
+                    stop=(g == GROUPS - 1),
+                )
+
+        def finish(s):
+            y = sb([P, 512], F32, "y%d" % s)
+            cols = slice(512 * s, 512 * (s + 1))
+            if s == 3:
+                plain = sb([P, 512], F32, "plain")
+                nc.scalar.copy(out=plain[:], in_=acc[s][:])
+                nc.gpsimd.tensor_tensor(out=y[:], in0=plain[:], in1=map_bias[:, cols], op=ADD)
+            else:
+                nc.vector.tensor_tensor(out=y[:], in0=acc[s][:], in1=map_bias[:, cols], op=ADD)
+            nc.sync.dma_start(out=out.rearrange("b c s -> (b c) s")[:, cols], in_=y[:])
+
+        for u in range(8):
+            widen(u)
+            turn(u)
+            if u < 4:
+                w_group(u)
+            h_out(u)
+            if u >= 2:
+                h_quant(u - 2)
+                if u < 6:
+                    w_quant(u - 2)
+            if u == 6:
+                decode(0, range(8))
+        decode(1, range(4))
+        x_bias(0)
+        x_bias(1)
+        h_quant(6)
+        x_turn(0)
+        x_turn(1)
+        h_quant(7)
+        x_out(0)
+        x_out(1)
+        decode(1, range(4, 8))
+        x_quant(0)
+        x_quant(1)
+        time_map(0)
+        time_map(1)
+        x_bias(2)
+        x_bias(3)
+        x_turn(2)
+        x_turn(3)
+        x_out(2)
+        x_out(3)
+        x_quant(2)
+        x_quant(3)
+        time_map(2)
+        time_map(3)
+        for s in range(4):
+            finish(s)

@@ -25,6 +25,16 @@ HALF = 64
 FLOPS = 2 * MODELS * BC * PATCHES * D * P + 2 * BC * T * T
 
 
+ORDER = """
+    D.0 sct W.0 D.1 M.0.1 M.0.0 M.2.1 T.0.1 M.1.1 T.0.0 M.2.0 M.4.1 bt.0 M.3.0 D.3 T.2.1 T.1.1 M.5.1 T.2.0 
+    M.1.0 T.4.1 E.0 D.2 B.0 M.3.1 T.3.0 T.5.1 T.1.0 Q.0 E.2 T.3.1 E.3 C.0.0 M.4.0 W.2 C.0.1 Q.2 W.3 Q.3 E.1 
+    Q.1 T.4.0 bt.2 C.3.0 W.1 M.5.0 C.2.0 B.2 C.3.1 C.1.0 E.4 X.0 bt.1 C.1.1 M.6.0 xT.0 C.2.1 xE.0 M.6.1 T.5.0 
+    B.1 E.5 T.6.0 T.6.1 xQ.0 G.0.0 X.1 G.0.1 M.7.1 M.7.0 E.6 xT.1 xE.1 G.0.2 T.7.1 Q.5 Q.4 E.7.1 T.7.0 C.5.0 
+    C.5.1 C.4.0 Q.6 E.7.0 C.6.1 C.6.0 Q.7 C.7.0 xQ.1 C.4.1 C.7.1 X.2 G.1.0 G.0.3 X.3 xT.2 G.1.1 xE.2 xT.3 
+    G.1.3 xE.3 xQ.2 G.2.1 G.2.3 xQ.3 G.3.1 F.1 G.3.3 F.3 G.2.0 G.1.2 G.3.0 G.2.2 F.0 G.3.2 F.2 
+"""
+
+
 def tile_model_pb_w8_kernel(tc, h_bytes, h_scale, dec_W, dec_b, map_W_words, map_W_scales, map_b, out):
     nc = tc.nc
 
@@ -36,12 +46,11 @@ def tile_model_pb_w8_kernel(tc, h_bytes, h_scale, dec_W, dec_b, map_W_words, map
         def sb(shape, dtype, name):
             return keep.tile(shape, dtype, name=name, align_bytes=64)
 
-        def bank(i, shape, name):
-            return psum.tile(shape, F32, name=name, tag="bank%d" % i)
+        def bank(i, shape, name, dtype=F32):
+            return psum.tile(shape, dtype, name=name, tag="bank%d" % i)
 
-        scale = sb([P, 2, D], F32, "scale")
-        nc.sync.dma_start(out=scale[:, 0], in_=h_scale.rearrange("a b c d k -> (a b c d k)").partition_broadcast(P))
-        nc.scalar.copy(out=scale[:, 1], in_=scale[:, 0])
+        scale_col = sb([P, 4], F32, "scale_col")
+        nc.sync.dma_start(out=scale_col[:], in_=h_scale.rearrange("a b c d (m p) -> p (a b c d m)", p=P))
 
         h_view = h_bytes.rearrange("n b c l d -> (b c) l n d")
         hb = {}
@@ -59,64 +68,92 @@ def tile_model_pb_w8_kernel(tc, h_bytes, h_scale, dec_W, dec_b, map_W_words, map
             nc.sync.dma_start(out=t[:], in_=dec_W[n0 : n0 + 2].rearrange("n (p j) w -> p n j w", j=4))
             w_raw[n0 // 2] = t
 
-        load_h(0, 1)
         load_w(0)
-        load_h(1, 2)
+        load_h(0, 1)
         load_w(2)
+        load_h(1, 2)
         load_h(2, 4)
         load_w(4)
         load_w(6)
-        load_h(4, 8)
 
         ident = sb([P, P], F32, "ident")
         make_identity(nc, ident[:])
+        rows = sb([P, T + MODELS * P], BF16, "rows")
+        nc.gpsimd.memset(rows[:].bitcast(I32), 0)
         wsc = sb([P, T], U8, "wsc")
         nc.gpsimd.memset(wsc[:].bitcast(I32), 0)
+        ones = sb([P, P], BF16, "ones")
+        nc.gpsimd.memset(ones[:], 1.0)
+        nc.sync.dma_start(out=rows[0:1, 0 : MODELS * P], in_=dec_b.rearrange("(o n) p -> o (n p)", o=1))
+        nc.sync.dma_start(out=rows[0:1, MODELS * P :], in_=map_b.rearrange("(o s) -> o s", o=1))
+        load_h(4, 8)
         for q in range(4):
             nc.sync.dma_start(
                 out=wsc[32 * q : 32 * q + 16, :].bitcast(I32),
                 in_=map_W_scales[:, 4 * q : 4 * q + 4, :].bitcast(I32),
             )
-        dec_bias = sb([P, MODELS, P], BF16, "dec_bias")
-        nc.sync.dma_start(
-            out=dec_bias[:].rearrange("b n p -> b (n p)"),
-            in_=dec_b.rearrange("n p -> (n p)").partition_broadcast(P),
-        )
         ww = []
         for g in range(GROUPS):
             t = sb([P, T], I32, "ww%d" % g)
             nc.sync.dma_start(out=t[:], in_=map_W_words[g].rearrange("p n t -> p (n t)").bitcast(I32))
             ww.append(t)
-        map_bias = sb([P, T], BF16, "map_bias")
-        nc.sync.dma_start(out=map_bias[:], in_=map_b.partition_broadcast(P))
+        scale = sb([P, D], F32, "scale")
+        bias = sb([P, T + MODELS * P], BF16, "bias")
+        dec_bias = bias[:, 0 : MODELS * P].rearrange("b (n p) -> b n p", n=MODELS)
+        map_bias = bias[:, MODELS * P :]
 
         hx, ht, hg, hc, hs = {}, {}, {}, {}, {}
         wg, wc, ws = {}, {}, {}
         x_ps, xb, xt, xg, xc, xs = {}, {}, {}, {}, {}, {}
         acc = {}
 
-        def widen(u):
-            hx[u] = sb([P, 2, D], BF16, "hx%d" % u)
-            nc.vector.tensor_tensor(
-                out=hx[u][:].rearrange("b i d -> b (i d)"),
-                in0=hb[u].rearrange("b i d -> b (i d)").bitcast(FP8),
-                in1=scale[:].rearrange("b i d -> b (i d)"),
-                op=MULT,
-            )
+        bias_ps = {}
 
-        def turn(u):
-            ht[u] = bank(u % 4, [P, 2, 2, P], "ht%d" % u)
-            for i in range(2):
-                words = hx[u][:, i].bitcast(F32)
-                for e in range(2):
-                    nc.tensor.transpose(ht[u][:, i, e], words[:, e::2], ident[:])
+        def spread_scale():
+            ps = bank(0, [P, D], "scale_ps")
+            for m in range(4):
+                nc.tensor.transpose(ps[:, m * P : (m + 1) * P], scale_col[:, m : m + 1].to_broadcast([P, P]), ident[:])
+            nc.scalar.copy(out=scale[:], in_=ps[:])
 
-        def h_out(u):
-            hg[u] = sb([P, 2, P, 4], BF16, "hg%d" % u)
-            nc.scalar.copy(
-                out=hg[u][:].rearrange("p i r k -> p (i r k)").bitcast(F32).rearrange("p (i r e) -> p i r e", i=2, e=2),
-                in_=ht[u][:].rearrange("p i e r -> p i r e"),
-            )
+        def spread_bias(b):
+            bias_ps[b] = bank((2, 7, 6)[b], [P, 1024], "bias_ps%d" % b, BF16)
+            for c in range(2):
+                nc.tensor.matmul(
+                    bias_ps[b][:, 512 * c : 512 * (c + 1)],
+                    ones[:],
+                    rows[:, 1024 * b + 512 * c : 1024 * b + 512 * (c + 1)],
+                    start=True,
+                    stop=True,
+                )
+
+        def bias_out(b):
+            nc.scalar.copy(out=bias[:, 1024 * b : 1024 * (b + 1)], in_=bias_ps[b][:])
+
+        def widen(u, i):
+            if u not in hx:
+                hx[u] = sb([P, 2, D], BF16, "hx%d" % u)
+            nc.vector.tensor_tensor(out=hx[u][:, i], in0=hb[u][:, i].bitcast(FP8), in1=scale[:], op=MULT)
+
+        def turn(u, i):
+            if u < 7:
+                if u not in ht:
+                    ht[u] = bank(4 + u if u < 4 else u % 2, [P, 2, 2, P], "ht%d" % u)
+                dst = ht[u][:, i]
+            else:
+                ht[u, i] = bank(1 - i, [P, 2, P], "ht%d_%d" % (u, i))
+                dst = ht[u, i][:]
+            words = hx[u][:, i].bitcast(F32)
+            for e in range(2):
+                nc.tensor.transpose(dst[:, e], words[:, e::2], ident[:])
+
+        def h_out(u, i=None):
+            if u not in hg:
+                hg[u] = sb([P, 2, P, 4], BF16, "hg%d" % u)
+            to = hg[u][:].rearrange("p i r k -> p (i r k)").bitcast(F32).rearrange("p (i r e) -> p i r e", i=2, e=2)
+            if i is None:
+                nc.scalar.copy(out=to, in_=ht[u][:].rearrange("p i e r -> p i r e"))
+            else:
+                nc.scalar.copy(out=to[:, i], in_=ht[u, i][:].rearrange("p e r -> p r e"))
 
         def h_quant(u):
             hc[u] = sb([P, 2 * P], U32, "hc%d" % u)
@@ -125,27 +162,30 @@ def tile_model_pb_w8_kernel(tc, h_bytes, h_scale, dec_W, dec_b, map_W_words, map
 
         def w_group(j):
             wg[j] = sb([P, 2, P, 4], BF16, "wg%d" % j)
-            nc.scalar.copy(out=wg[j][:], in_=w_raw[j][:].rearrange("p n j w -> p n w j"))
+            if j == 0:
+                nc.vector.tensor_copy(out=wg[j][:], in_=w_raw[j][:].rearrange("p n j w -> p n w j"))
+            else:
+                nc.scalar.copy(out=wg[j][:], in_=w_raw[j][:].rearrange("p n j w -> p n w j"))
 
         def w_quant(j):
             wc[j] = sb([P, 2 * P], U32, "wc%d" % j)
             ws[j] = sb([P, 2 * P], U8, "ws%d" % j)
             nc.vector.quantize_mx(out=wc[j][:].bitcast(FP8X4), scales=ws[j][:], in_=wg[j][:].rearrange("p i r k -> p (i r k)"))
 
-        def decode(l, models):
-            for half in range(2):
-                g = 2 * l + half
-                if g not in x_ps:
-                    x_ps[g] = bank(4 + half, [P, MODELS, HALF], "x_ps%d" % g)
-                for n in models:
-                    u, i = 4 * l + n // 2, n % 2
+        def decode(u, half):
+            l, j = u // 4, u % 4
+            g = 2 * l + half
+            if g not in x_ps:
+                x_ps[g] = bank(2 + half, [P, MODELS, HALF], "x_ps%d" % g)
+            if True:
+                for i in range(2):
                     cols = slice(i * P + half * HALF, i * P + half * HALF + HALF)
                     nc.tensor.matmul_mx(
-                        out=x_ps[g][:, n],
+                        out=x_ps[2 * l + half][:, 2 * j + i],
                         lhsT=hc[u][:, i * P : (i + 1) * P].bitcast(FP8X4),
                         lhsT_scale=hs[u][:, i * P : (i + 1) * P],
-                        rhs=wc[n // 2][:, cols].bitcast(FP8X4),
-                        rhs_scale=ws[n // 2][:, cols],
+                        rhs=wc[j][:, cols].bitcast(FP8X4),
+                        rhs_scale=ws[j][:, cols],
                         start=True,
                         stop=True,
                     )
@@ -161,7 +201,7 @@ def tile_model_pb_w8_kernel(tc, h_bytes, h_scale, dec_W, dec_b, map_W_words, map
             )
 
         def x_turn(g):
-            xt[g] = bank(6 + g % 2, [P, 2, P], "xt%d" % g)
+            xt[g] = bank(g % 2, [P, 2, P], "xt%d" % g)
             words = xb[g][:].rearrange("b p n -> b (p n)").bitcast(F32)
             for e in range(2):
                 nc.tensor.transpose(xt[g][:, e], words[:, e::2], ident[:])
@@ -178,67 +218,31 @@ def tile_model_pb_w8_kernel(tc, h_bytes, h_scale, dec_W, dec_b, map_W_words, map
             xs[g] = sb([P, P], U8, "xs%d" % g)
             nc.vector.quantize_mx(out=xc[g][:].bitcast(FP8X4), scales=xs[g][:], in_=xg[g][:].rearrange("p r k -> p (r k)"))
 
-        def time_map(g):
-            for s in (3, 0, 1, 2):
-                if g == 0:
-                    acc[s] = bank(s, [P, 512], "acc%d" % s)
-                cols = slice(512 * s, 512 * (s + 1))
-                nc.tensor.matmul_mx(
-                    out=acc[s][:],
-                    lhsT=xc[g][:].bitcast(FP8X4),
-                    lhsT_scale=xs[g][:],
-                    rhs=ww[g][:, cols].bitcast(FP8X4),
-                    rhs_scale=wsc[4 * g : P, cols],
-                    start=(g == 0),
-                    stop=(g == GROUPS - 1),
-                )
+        def time_map(g, s):
+            if g == 0:
+                acc[s] = bank(4 + s, [P, 512], "acc%d" % s)
+            cols = slice(512 * s, 512 * (s + 1))
+            nc.tensor.matmul_mx(
+                out=acc[s][:],
+                lhsT=xc[g][:].bitcast(FP8X4),
+                lhsT_scale=xs[g][:],
+                rhs=ww[g][:, cols].bitcast(FP8X4),
+                rhs_scale=wsc[4 * g : P, cols],
+                start=(g == 0),
+                stop=(g == GROUPS - 1),
+            )
 
         def finish(s):
             y = sb([P, 512], F32, "y%d" % s)
             cols = slice(512 * s, 512 * (s + 1))
-            if s == 3:
-                plain = sb([P, 512], F32, "plain")
-                nc.scalar.copy(out=plain[:], in_=acc[s][:])
-                nc.gpsimd.tensor_tensor(out=y[:], in0=plain[:], in1=map_bias[:, cols], op=ADD)
-            else:
-                nc.vector.tensor_tensor(out=y[:], in0=acc[s][:], in1=map_bias[:, cols], op=ADD)
+            nc.vector.tensor_tensor(out=y[:], in0=acc[s][:], in1=map_bias[:, cols], op=ADD)
             nc.sync.dma_start(out=out.rearrange("b c s -> (b c) s")[:, cols], in_=y[:])
 
-        for u in range(8):
-            widen(u)
-            turn(u)
-            if u < 4:
-                w_group(u)
-            h_out(u)
-            if u >= 2:
-                h_quant(u - 2)
-                if u < 6:
-                    w_quant(u - 2)
-            if u == 6:
-                decode(0, range(8))
-        decode(1, range(4))
-        x_bias(0)
-        x_bias(1)
-        h_quant(6)
-        x_turn(0)
-        x_turn(1)
-        h_quant(7)
-        x_out(0)
-        x_out(1)
-        decode(1, range(4, 8))
-        x_quant(0)
-        x_quant(1)
-        time_map(0)
-        time_map(1)
-        x_bias(2)
-        x_bias(3)
-        x_turn(2)
-        x_turn(3)
-        x_out(2)
-        x_out(3)
-        x_quant(2)
-        x_quant(3)
-        time_map(2)
-        time_map(3)
-        for s in range(4):
-            finish(s)
+        for step in ORDER.split():
+            a = [int(c) for c in step.split(".")[1:]]
+            STEPS = {
+                "sct": spread_scale, "bt": spread_bias, "B": bias_out, "D": w_group, "W": w_quant, "M": widen, "T": turn,
+                "E": h_out, "Q": h_quant, "C": decode, "X": x_bias, "xT": x_turn, "xE": x_out, "xQ": x_quant,
+                "G": time_map, "F": finish,
+            }
+            STEPS[step.split(".")[0]](*a)

@@ -26,12 +26,12 @@ FLOPS = 2 * MODELS * BC * PATCHES * D * P + 2 * BC * T * T
 
 
 ORDER = """
-    D.0 sct W.0 D.1 M.0.1 M.0.0 M.2.1 T.0.1 M.1.1 T.0.0 M.2.0 M.4.1 bt.0 M.3.0 D.3 T.2.1 T.1.1 M.5.1 T.2.0 
-    M.1.0 T.4.1 E.0 D.2 B.0 M.3.1 T.3.0 T.5.1 T.1.0 Q.0 E.2 T.3.1 E.3 C.0.0 M.4.0 W.2 C.0.1 Q.2 W.3 Q.3 E.1 
-    Q.1 T.4.0 bt.2 C.3.0 W.1 M.5.0 C.2.0 B.2 C.3.1 C.1.0 E.4 X.0 bt.1 C.1.1 M.6.0 xT.0 C.2.1 xE.0 M.6.1 T.5.0 
-    B.1 E.5 T.6.0 T.6.1 xQ.0 G.0.0 X.1 G.0.1 M.7.1 M.7.0 E.6 xT.1 xE.1 G.0.2 T.7.1 Q.5 Q.4 E.7.1 T.7.0 C.5.0 
-    C.5.1 C.4.0 Q.6 E.7.0 C.6.1 C.6.0 Q.7 C.7.0 xQ.1 C.4.1 C.7.1 X.2 G.1.0 G.0.3 X.3 xT.2 G.1.1 xE.2 xT.3 
-    G.1.3 xE.3 xQ.2 G.2.1 G.2.3 xQ.3 G.3.1 F.1 G.3.3 F.3 G.2.0 G.1.2 G.3.0 G.2.2 F.0 G.3.2 F.2 
+    D.0 sct W.0 M.0.0 M.1.1 M.1.0 T.0.0 T.1.1 M.2.1 D.1 D.2 bt.0 M.3.0 M.0.1 M.3.1 T.1.0 D.3 T.2.1 T.3.0 M.4.0 
+    T.0.1 M.2.0 W.2 B.0 bt.1 E.1 T.3.1 M.4.1 K E.0 Q.0 T.2.0 W.1 E.3 Q.1 E.2 T.4.0 Q.2 bt.2 B.1 M.5.0 T.4.1 
+    C.0.1 Q.3 C.0.0 C.2.0 W.3 C.1.0 C.2.1 C.3.0 E.4 B.2 C.1.1 M.5.1 C.3.1 X.0 M.6.0 T.5.1 M.6.1 xT.0 T.5.0 
+    xE.0 T.6.0 T.6.1 X.1 E.5 xT.1 xQ.0 G.0.0 M.7.0 G.0.2 xE.1 G.0.1 M.7.1 T.7.0 E.6 Q.5 T.7.1 E.7.0 Q.6 G.0.3 
+    C.5.1 Q.4 E.7.1 C.6.0 C.5.0 Q.7 C.4.0 xQ.1 C.7.0 C.7.1 C.4.1 X.2 C.6.1 G.1.1 G.1.2 xT.2 xE.2 X.3 xT.3 
+    G.1.0 xQ.2 xE.3 xQ.3 G.1.3 G.2.0 G.2.2 G.3.0 F.0 G.2.1 G.3.2 F.2 G.3.1 G.2.3 F.1 G.3.3 F.3 
 """
 
 
@@ -50,7 +50,7 @@ def tile_model_pb_w8_kernel(tc, h_bytes, h_scale, dec_W, dec_b, map_W_words, map
             return psum.tile(shape, dtype, name=name, tag="bank%d" % i)
 
         scale_col = sb([P, 4], F32, "scale_col")
-        nc.sync.dma_start(out=scale_col[:], in_=h_scale.rearrange("a b c d (m p) -> p (a b c d m)", p=P))
+        nc.sync.dma_start(out=scale_col[:], in_=h_scale.rearrange("a b c d (p j) -> p (a b c d j)", p=P))
 
         h_view = h_bytes.rearrange("n b c l d -> (b c) l n d")
         hb = {}
@@ -113,10 +113,10 @@ def tile_model_pb_w8_kernel(tc, h_bytes, h_scale, dec_W, dec_b, map_W_words, map
             ps = bank(0, [P, D], "scale_ps")
             for m in range(4):
                 nc.tensor.transpose(ps[:, m * P : (m + 1) * P], scale_col[:, m : m + 1].to_broadcast([P, P]), ident[:])
-            nc.scalar.copy(out=scale[:], in_=ps[:])
+            nc.scalar.copy(out=scale[:].rearrange("b (p j) -> b p j", j=4), in_=ps[:].rearrange("b (j p) -> b p j", j=4))
 
         def spread_bias(b):
-            bias_ps[b] = bank((2, 7, 6)[b], [P, 1024], "bias_ps%d" % b, BF16)
+            bias_ps[b] = bank((2, 3, 1)[b], [P, 1024], "bias_ps%d" % b, BF16)
             for c in range(2):
                 nc.tensor.matmul(
                     bias_ps[b][:, 512 * c : 512 * (c + 1)],
@@ -125,6 +125,9 @@ def tile_model_pb_w8_kernel(tc, h_bytes, h_scale, dec_W, dec_b, map_W_words, map
                     start=True,
                     stop=True,
                 )
+
+        def keep_warm():
+            nc.tensor.matmul(bank(0, [P, 512], "warm")[:], ones[:], rows[:, 0:512], start=True, stop=True)
 
         def bias_out(b):
             nc.scalar.copy(out=bias[:, 1024 * b : 1024 * (b + 1)], in_=bias_ps[b][:])
@@ -162,10 +165,13 @@ def tile_model_pb_w8_kernel(tc, h_bytes, h_scale, dec_W, dec_b, map_W_words, map
 
         def w_group(j):
             wg[j] = sb([P, 2, P, 4], BF16, "wg%d" % j)
-            if j == 0:
-                nc.vector.tensor_copy(out=wg[j][:], in_=w_raw[j][:].rearrange("p n j w -> p n w j"))
-            else:
-                nc.scalar.copy(out=wg[j][:], in_=w_raw[j][:].rearrange("p n j w -> p n w j"))
+            for n in range(2):
+                to = wg[j][:, n].rearrange("p (c i) t -> p c t i", i=4)
+                of = w_raw[j][:, n].rearrange("p t (c i) -> p c t i", i=4)
+                if j == 0:
+                    nc.vector.tensor_copy(out=to, in_=of)
+                else:
+                    nc.scalar.copy(out=to, in_=of)
 
         def w_quant(j):
             wc[j] = sb([P, 2 * P], U32, "wc%d" % j)
@@ -192,19 +198,16 @@ def tile_model_pb_w8_kernel(tc, h_bytes, h_scale, dec_W, dec_b, map_W_words, map
 
         def x_bias(g):
             half = g % 2
-            xb[g] = sb([P, HALF, MODELS], BF16, "xb%d" % g)
-            nc.vector.tensor_tensor(
-                out=xb[g][:],
-                in0=x_ps[g][:].rearrange("b n p -> b p n"),
-                in1=dec_bias[:, :, half * HALF : (half + 1) * HALF].rearrange("b n p -> b p n"),
-                op=ADD,
-            )
+            xb[g] = sb([P, 2, HALF, 2, 2], BF16, "xb%d" % g)
+            ps = x_ps[g][:].rearrange("b (q u e) p -> b u p q e", q=2, u=2)
+            bs = dec_bias[:, :, half * HALF : (half + 1) * HALF].rearrange("b (q u e) p -> b u p q e", q=2, u=2)
+            for u in range(2):
+                nc.vector.tensor_tensor(out=xb[g][:, u], in0=ps[:, u], in1=bs[:, u], op=ADD)
 
         def x_turn(g):
             xt[g] = bank(g % 2, [P, 2, P], "xt%d" % g)
-            words = xb[g][:].rearrange("b p n -> b (p n)").bitcast(F32)
-            for e in range(2):
-                nc.tensor.transpose(xt[g][:, e], words[:, e::2], ident[:])
+            for u in range(2):
+                nc.tensor.transpose(xt[g][:, u], xb[g][:, u].rearrange("b p q e -> b (p q e)").bitcast(F32), ident[:])
 
         def x_out(g):
             xg[g] = sb([P, P, 4], BF16, "xg%d" % g)
@@ -234,15 +237,19 @@ def tile_model_pb_w8_kernel(tc, h_bytes, h_scale, dec_W, dec_b, map_W_words, map
 
         def finish(s):
             y = sb([P, 512], F32, "y%d" % s)
-            cols = slice(512 * s, 512 * (s + 1))
-            nc.vector.tensor_tensor(out=y[:], in0=acc[s][:], in1=map_bias[:, cols], op=ADD)
-            nc.sync.dma_start(out=out.rearrange("b c s -> (b c) s")[:, cols], in_=y[:])
+            parts = 2 if s == 3 else 1
+            width = 512 // parts
+            for k in range(parts):
+                here = slice(width * k, width * (k + 1))
+                cols = slice(512 * s + width * k, 512 * s + width * (k + 1))
+                nc.vector.tensor_tensor(out=y[:, here], in0=acc[s][:, here], in1=map_bias[:, cols], op=ADD)
+                nc.sync.dma_start(out=out.rearrange("b c s -> (b c) s")[:, cols], in_=y[:, here])
 
         for step in ORDER.split():
             a = [int(c) for c in step.split(".")[1:]]
             STEPS = {
                 "sct": spread_scale, "bt": spread_bias, "B": bias_out, "D": w_group, "W": w_quant, "M": widen, "T": turn,
                 "E": h_out, "Q": h_quant, "C": decode, "X": x_bias, "xT": x_turn, "xE": x_out, "xQ": x_quant,
-                "G": time_map, "F": finish,
+                "K": keep_warm, "G": time_map, "F": finish,
             }
             STEPS[step.split(".")[0]](*a)

from contextlib import ExitStack

import concourse.mybir as mybir
from concourse.masks import make_identity

F32 = mybir.dt.float32
BF16 = mybir.dt.bfloat16
I32 = mybir.dt.int32
U32 = mybir.dt.uint32
U8 = mybir.dt.uint8
FP8 = mybir.dt.float8_e4m3fn
FP8X4 = mybir.dt.float8_e4m3fn_x4
MULT = mybir.AluOpType.mult
ADD = mybir.AluOpType.add

P = 128
MODELS = 8
D = 512
T = 2048
BC = 128
PATCHES = 2
GROUPS = T // 512
HALF = 64

FLOPS = 2 * MODELS * BC * PATCHES * D * P + 2 * BC * T * T


ORDER = """
    D.0 sct W.0 M.0.0 M.1.1 M.1.0 T.0.0 T.1.1 M.2.1 D.1 D.2 bt.0 M.3.0 M.0.1 M.3.1 T.1.0 D.3 T.2.1 T.3.0 M.4.0 
    T.0.1 M.2.0 W.2 B.0 bt.1 E.1 T.3.1 M.4.1 K E.0 Q.0 T.2.0 W.1 E.3 Q.1 E.2 T.4.0 Q.2 bt.2 B.1 M.5.0 T.4.1 
    C.0.1 Q.3 C.0.0 C.2.0 W.3 C.1.0 C.2.1 C.3.0 E.4 B.2 C.1.1 M.5.1 C.3.1 X.0 M.6.0 T.5.1 M.6.1 xT.0 T.5.0 
    xE.0 T.6.0 T.6.1 X.1 E.5 xT.1 xQ.0 G.0.0 M.7.0 G.0.2 xE.1 G.0.1 M.7.1 T.7.0 E.6 Q.5 T.7.1 E.7.0 Q.6 G.0.3 
    C.5.1 Q.4 E.7.1 C.6.0 C.5.0 Q.7 C.4.0 xQ.1 C.7.0 C.7.1 C.4.1 X.2 C.6.1 G.1.1 G.1.2 xT.2 xE.2 X.3 xT.3 
    G.1.0 xQ.2 xE.3 xQ.3 G.1.3 G.2.0 G.2.2 G.3.0 F.0 G.2.1 G.3.2 F.2 G.3.1 G.2.3 F.1 G.3.3 F.3 
"""


def tile_model_pb_w8_kernel(tc, h_bytes, h_scale, dec_W, dec_b, map_W_words, map_W_scales, map_b, out):
    nc = tc.nc

    with ExitStack() as ctx:
        keep = ctx.enter_context(tc.tile_pool(name="keep", bufs=1))
        psum = ctx.enter_context(tc.psum_pool(name="psum", bufs=1))
        ctx.enter_context(tc.manual_schedule())

        def sb(shape, dtype, name):
            return keep.tile(shape, dtype, name=name, align_bytes=64)

        def bank(i, shape, name, dtype=F32):
            return psum.tile(shape, dtype, name=name, tag="bank%d" % i)

        scale_col = sb([P, 4], F32, "scale_col")
        nc.sync.dma_start(out=scale_col[:], in_=h_scale.rearrange("a b c d (p j) -> p (a b c d j)", p=P))

        h_view = h_bytes.rearrange("n b c l d -> (b c) l n d")
        hb = {}
        w_raw = {}

        def load_h(u0, u1):
            l, n0 = u0 // 4, 2 * (u0 % 4)
            t = sb([P, 2 * (u1 - u0), D], U8, "hb%d" % u0)
            nc.sync.dma_start(out=t[:], in_=h_view[:, l, n0 : n0 + 2 * (u1 - u0)])
            for u in range(u0, u1):
                hb[u] = t[:, 2 * (u - u0) : 2 * (u - u0) + 2]

        def load_w(n0):
            t = sb([P, 2, 4, P], BF16, "w_raw%d" % n0)
            nc.sync.dma_start(out=t[:], in_=dec_W[n0 : n0 + 2].rearrange("n (p j) w -> p n j w", j=4))
            w_raw[n0 // 2] = t

        load_w(0)
        load_h(0, 1)
        load_w(2)
        load_h(1, 2)
        load_h(2, 4)
        load_w(4)
        load_w(6)

        ident = sb([P, P], F32, "ident")
        make_identity(nc, ident[:])
        rows = sb([P, T + MODELS * P], BF16, "rows")
        nc.gpsimd.memset(rows[:].bitcast(I32), 0)
        wsc = sb([P, T], U8, "wsc")
        nc.gpsimd.memset(wsc[:].bitcast(I32), 0)
        ones = sb([P, P], BF16, "ones")
        nc.gpsimd.memset(ones[:], 1.0)
        nc.sync.dma_start(out=rows[0:1, 0 : MODELS * P], in_=dec_b.rearrange("(o n) p -> o (n p)", o=1))
        nc.sync.dma_start(out=rows[0:1, MODELS * P :], in_=map_b.rearrange("(o s) -> o s", o=1))
        load_h(4, 8)
        for q in range(4):
            nc.sync.dma_start(
                out=wsc[32 * q : 32 * q + 16, :].bitcast(I32),
                in_=map_W_scales[:, 4 * q : 4 * q + 4, :].bitcast(I32),
            )
        ww = []
        for g in range(GROUPS):
            t = sb([P, T], I32, "ww%d" % g)
            nc.sync.dma_start(out=t[:], in_=map_W_words[g].rearrange("p n t -> p (n t)").bitcast(I32))
            ww.append(t)
        scale = sb([P, D], F32, "scale")
        bias = sb([P, T + MODELS * P], BF16, "bias")
        dec_bias = bias[:, 0 : MODELS * P].rearrange("b (n p) -> b n p", n=MODELS)
        map_bias = bias[:, MODELS * P :]

        hx, ht, hg, hc, hs = {}, {}, {}, {}, {}
        wg, wc, ws = {}, {}, {}
        x_ps, xb, xt, xg, xc, xs = {}, {}, {}, {}, {}, {}
        acc = {}

        bias_ps = {}

        def spread_scale():
            ps = bank(0, [P, D], "scale_ps")
            for m in range(4):
                nc.tensor.transpose(ps[:, m * P : (m + 1) * P], scale_col[:, m : m + 1].to_broadcast([P, P]), ident[:])
            nc.scalar.copy(out=scale[:].rearrange("b (p j) -> b p j", j=4), in_=ps[:].rearrange("b (j p) -> b p j", j=4))

        def spread_bias(b):
            bias_ps[b] = bank((2, 3, 1)[b], [P, 1024], "bias_ps%d" % b, BF16)
            for c in range(2):
                nc.tensor.matmul(
                    bias_ps[b][:, 512 * c : 512 * (c + 1)],
                    ones[:],
                    rows[:, 1024 * b + 512 * c : 1024 * b + 512 * (c + 1)],
                    start=True,
                    stop=True,
                )

        def keep_warm():
            nc.tensor.matmul(bank(0, [P, 512], "warm")[:], ones[:], rows[:, 0:512], start=True, stop=True)

        def bias_out(b):
            nc.scalar.copy(out=bias[:, 1024 * b : 1024 * (b + 1)], in_=bias_ps[b][:])

        def widen(u, i):
            if u not in hx:
                hx[u] = sb([P, 2, D], BF16, "hx%d" % u)
            nc.vector.tensor_tensor(out=hx[u][:, i], in0=hb[u][:, i].bitcast(FP8), in1=scale[:], op=MULT)

        def turn(u, i):
            if u < 7:
                if u not in ht:
                    ht[u] = bank(4 + u if u < 4 else u % 2, [P, 2, 2, P], "ht%d" % u)
                dst = ht[u][:, i]
            else:
                ht[u, i] = bank(1 - i, [P, 2, P], "ht%d_%d" % (u, i))
                dst = ht[u, i][:]
            words = hx[u][:, i].bitcast(F32)
            for e in range(2):
                nc.tensor.transpose(dst[:, e], words[:, e::2], ident[:])

        def h_out(u, i=None):
            if u not in hg:
                hg[u] = sb([P, 2, P, 4], BF16, "hg%d" % u)
            to = hg[u][:].rearrange("p i r k -> p (i r k)").bitcast(F32).rearrange("p (i r e) -> p i r e", i=2, e=2)
            if i is None:
                nc.scalar.copy(out=to, in_=ht[u][:].rearrange("p i e r -> p i r e"))
            else:
                nc.scalar.copy(out=to[:, i], in_=ht[u, i][:].rearrange("p e r -> p r e"))

        def h_quant(u):
            hc[u] = sb([P, 2 * P], U32, "hc%d" % u)
            hs[u] = sb([P, 2 * P], U8, "hs%d" % u)
            nc.vector.quantize_mx(out=hc[u][:].bitcast(FP8X4), scales=hs[u][:], in_=hg[u][:].rearrange("p i r k -> p (i r k)"))

        def w_group(j):
            wg[j] = sb([P, 2, P, 4], BF16, "wg%d" % j)
            for n in range(2):
                to = wg[j][:, n].rearrange("p (c i) t -> p c t i", i=4)
                of = w_raw[j][:, n].rearrange("p t (c i) -> p c t i", i=4)
                if j == 0:
                    nc.vector.tensor_copy(out=to, in_=of)
                else:
                    nc.scalar.copy(out=to, in_=of)

        def w_quant(j):
            wc[j] = sb([P, 2 * P], U32, "wc%d" % j)
            ws[j] = sb([P, 2 * P], U8, "ws%d" % j)
            nc.vector.quantize_mx(out=wc[j][:].bitcast(FP8X4), scales=ws[j][:], in_=wg[j][:].rearrange("p i r k -> p (i r k)"))

        def decode(u, half):
            l, j = u // 4, u % 4
            g = 2 * l + half
            if g not in x_ps:
                x_ps[g] = bank(2 + half, [P, MODELS, HALF], "x_ps%d" % g)
            if True:
                for i in range(2):
                    cols = slice(i * P + half * HALF, i * P + half * HALF + HALF)
                    nc.tensor.matmul_mx(
                        out=x_ps[2 * l + half][:, 2 * j + i],
                        lhsT=hc[u][:, i * P : (i + 1) * P].bitcast(FP8X4),
                        lhsT_scale=hs[u][:, i * P : (i + 1) * P],
                        rhs=wc[j][:, cols].bitcast(FP8X4),
                        rhs_scale=ws[j][:, cols],
                        start=True,
                        stop=True,
                    )

        def x_bias(g):
            half = g % 2
            xb[g] = sb([P, 2, HALF, 2, 2], BF16, "xb%d" % g)
            ps = x_ps[g][:].rearrange("b (q u e) p -> b u p q e", q=2, u=2)
            bs = dec_bias[:, :, half * HALF : (half + 1) * HALF].rearrange("b (q u e) p -> b u p q e", q=2, u=2)
            for u in range(2):
                nc.vector.tensor_tensor(out=xb[g][:, u], in0=ps[:, u], in1=bs[:, u], op=ADD)

        def x_turn(g):
            xt[g] = bank(g % 2, [P, 2, P], "xt%d" % g)
            for u in range(2):
                nc.tensor.transpose(xt[g][:, u], xb[g][:, u].rearrange("b p q e -> b (p q e)").bitcast(F32), ident[:])

        def x_out(g):
            xg[g] = sb([P, P, 4], BF16, "xg%d" % g)
            nc.scalar.copy(
                out=xg[g][:].rearrange("p r k -> p (r k)").bitcast(F32).rearrange("p (r e) -> p r e", e=2),
                in_=xt[g][:].rearrange("p e r -> p r e"),
            )

        def x_quant(g):
            xc[g] = sb([P, P], U32, "xc%d" % g)
            xs[g] = sb([P, P], U8, "xs%d" % g)
            nc.vector.quantize_mx(out=xc[g][:].bitcast(FP8X4), scales=xs[g][:], in_=xg[g][:].rearrange("p r k -> p (r k)"))

        def time_map(g, s):
            if g == 0:
                acc[s] = bank(4 + s, [P, 512], "acc%d" % s)
            cols = slice(512 * s, 512 * (s + 1))
            nc.tensor.matmul_mx(
                out=acc[s][:],
                lhsT=xc[g][:].bitcast(FP8X4),
                lhsT_scale=xs[g][:],
                rhs=ww[g][:, cols].bitcast(FP8X4),
                rhs_scale=wsc[4 * g : P, cols],
                start=(g == 0),
                stop=(g == GROUPS - 1),
            )

        def finish(s):
            y = sb([P, 512], F32, "y%d" % s)
            parts = 2 if s == 3 else 1
            width = 512 // parts
            for k in range(parts):
                here = slice(width * k, width * (k + 1))
                cols = slice(512 * s + width * k, 512 * s + width * (k + 1))
                nc.vector.tensor_tensor(out=y[:, here], in0=acc[s][:, here], in1=map_bias[:, cols], op=ADD)
                nc.sync.dma_start(out=out.rearrange("b c s -> (b c) s")[:, cols], in_=y[:, here])

        for step in ORDER.split():
            a = [int(c) for c in step.split(".")[1:]]
            STEPS = {
                "sct": spread_scale, "bt": spread_bias, "B": bias_out, "D": w_group, "W": w_quant, "M": widen, "T": turn,
                "E": h_out, "Q": h_quant, "C": decode, "X": x_bias, "xT": x_turn, "xE": x_out, "xQ": x_quant,
                "K": keep_warm, "G": time_map, "F": finish,
            }
            STEPS[step.split(".")[0]](*a)
